import numpy as np
import ml_dtypes


def mxq(x, axis, fmt="e4m3"):
    dtype, down = {"e4m3": (ml_dtypes.float8_e4m3fn, 7), "e5m2": (ml_dtypes.float8_e5m2, 14)}[fmt]
    v = np.moveaxis(np.asarray(x, np.float32).astype(ml_dtypes.bfloat16).astype(np.float64), axis, -1)
    blocks = v.reshape(v.shape[:-1] + (-1, 32))
    amax = np.abs(blocks).max(-1, keepdims=True)
    byte = np.maximum(np.where(amax > 0, np.frexp(amax)[1] - 1 + 127, 0) - down, 1)
    scale = np.exp2(byte - 127.0)
    codes = (blocks / scale).astype(np.float32).astype(dtype).astype(np.float64)
    return np.moveaxis((codes * scale).reshape(v.shape), -1, axis)


WIDE = False


def mx_kscale(k):
    if not WIDE:
        return np.ones(k)
    levels = np.array([10, -10, 5, -5, 0])
    a = np.random.permutation(np.resize(levels, k // 512 * 4)).reshape(k // 512, 4)
    idx = np.arange(k)
    return np.exp2(a[idx // 512, idx % 128 // 32])


BF16 = ml_dtypes.bfloat16


def bf(x):
    return np.asarray(x, np.float32).astype(BF16)


def f64(x):
    return np.asarray(x).astype(np.float64)


E2M1 = np.array([0.0, 0.5, 1.0, 1.5, 2.0, 3.0, 4.0, 6.0, -0.0, -0.5, -1.0, -1.5, -2.0, -3.0, -4.0, -6.0])


def pack_weight(w, fmt):
    k, n = w.shape
    w = f64(bf(w)).reshape(k // 32, 32, n)
    amax = np.abs(w).max(1)
    if fmt == "e4m3":
        byte = np.frexp(amax)[1] - 1 + 127 - 7
    else:
        mant, ex = np.frexp(amax / 6.0)
        byte = np.where(mant > 0.5, ex, ex - 1) + 127
    byte = np.clip(np.where(amax > 0, byte, 1), 1, 254)
    scaled = (w * np.exp2(127.0 - byte)[:, None, :]).reshape(k, n).astype(np.float32)
    by_word = np.ascontiguousarray(scaled.reshape(k // 512, 128, 4, n).transpose(0, 1, 3, 2))
    if fmt == "e4m3":
        words = by_word.astype(ml_dtypes.float8_e4m3fn).view(np.uint8)
    else:
        c = by_word.astype(ml_dtypes.float4_e2m1fn).view(np.uint8) & 0xF
        words = c[..., 0::2] | (c[..., 1::2] << 4)
    return np.ascontiguousarray(words), np.ascontiguousarray(byte.astype(np.uint8).reshape(k // 512, 16, n))


def unpack_weight(words, scales, fmt):
    g, p, n, _ = words.shape
    if fmt == "e4m3":
        vals = np.ascontiguousarray(words).view(ml_dtypes.float8_e4m3fn).astype(np.float64)
    else:
        nib = np.empty((g, p, n, 4), np.uint8)
        nib[..., 0::2] = words & 0xF
        nib[..., 1::2] = words >> 4
        vals = E2M1[nib]
    vals = vals * np.repeat(np.exp2(scales.astype(np.float64) - 127.0), 8, axis=1)[..., None]
    return vals.transpose(0, 1, 3, 2).reshape(g * 512, n)


B, D, F, H = 256, 4, 2048, 2048
NAN_FRAC = 0.15
FMT = "e4m3"


def setup_inputs():
    t = mx_kscale(F)
    labels = np.random.standard_normal((B, D))
    labels = np.where(np.random.random((B, D)) < NAN_FRAC, np.nan, labels)
    emb_w = bf(np.random.standard_normal((D, H)) * 0.5)
    w1 = bf(np.random.standard_normal((D, F)))
    b1 = bf(np.random.standard_normal((D, F)) * 0.3 + np.log(t))
    w2 = np.random.standard_normal((D, H, F)) * 0.25 * np.sqrt(F) * t.mean() / t
    cat = np.ascontiguousarray(w2.swapaxes(1, 2)).reshape(-1, H)
    w2_words, w2_scales = pack_weight(cat, FMT)
    return {"labels": bf(labels),
            "emb_w": emb_w,
            "w1": w1,
            "b1": b1,
            "w2_words": w2_words,
            "w2_scales": w2_scales,
            "train": 0, "unconditioned": 0}


def reference(labels, emb_w, w1, b1, w2_words, w2_scales, train, unconditioned):
    labels, emb_w, w1, b1 = f64(labels), f64(emb_w), f64(w1), f64(b1)
    assert not train
    if unconditioned:
        drop = np.ones(labels.shape, dtype=bool)
    else:
        drop = np.isnan(labels)
    safe = np.where(drop, 0.0, labels)
    h1 = safe[:, :, None] * w1[None, :, :] + b1[None, :, :]
    e = np.exp(h1 - h1.max(-1, keepdims=True))
    s = e / e.sum(-1, keepdims=True)
    mlp = (mxq(s, 2, "e4m3").transpose(1, 0, 2) @ unpack_weight(w2_words, w2_scales, FMT).reshape(D, F, H)).transpose(1, 0, 2)
    emb = np.where(drop[:, :, None], emb_w[None, :, :], mlp)
    return emb.sum(axis=1)

@@ -1,0 +1,277 @@
+from contextlib import ExitStack
+
+import concourse.mybir as mybir
+from concourse.masks import make_identity
+
+F32 = mybir.dt.float32
+BF16 = mybir.dt.bfloat16
+I32 = mybir.dt.int32
+U32 = mybir.dt.uint32
+U8 = mybir.dt.uint8
+FP8X4 = mybir.dt.float8_e4m3fn_x4
+ALU = mybir.AluOpType
+ACT = mybir.ActivationFunctionType
+
+P = 128
+B, D, F, H = 256, 4, 2048, 2048
+B_TILES = B // P
+K_PASS = 4 * P
+PASSES = F // K_PASS
+N_TILE = 512
+N_TILES = H // N_TILE
+INFINITY_BITS = 0x7F800000
+
+ROW_ONE = D
+ROW_MISSING = D + 1
+
+UNITS = [(d, t) for t in range(B_TILES) for d in range(D)]
+
+FLOPS = 2 * B * D * F * H
+
+
+def tile_conditionembedder_w_e_kernel(
+    tc, labels, emb_w, w1, b1, w2_words, w2_scales, train, unconditioned, out
+):
+    nc = tc.nc
+    assert not train and not unconditioned
+
+    with ExitStack() as ctx:
+        keep = ctx.enter_context(tc.tile_pool(name="keep", bufs=1))
+        work = ctx.enter_context(tc.tile_pool(name="work", bufs=2))
+        small = ctx.enter_context(tc.tile_pool(name="small", bufs=4))
+        acc_pool = ctx.enter_context(tc.psum_pool(name="acc", bufs=1))
+        h1_pool = ctx.enter_context(tc.psum_pool(name="h1", bufs=2))
+        tr_pool = ctx.enter_context(tc.psum_pool(name="tr", bufs=2))
+
+        rows = keep.tile([P, D + 1, F], BF16)
+        w_words = keep.tile([P, D * PASSES, H], U32, align_bytes=64)
+        w_planes = keep.tile([P, D, H], U8, align_bytes=64)
+        s_words = keep.tile([P, B_TILES, D * PASSES, P], U32, align_bytes=64)
+        s_planes = keep.tile([P, B_TILES, D * PASSES, P], U8, align_bytes=64)
+        result = keep.tile([P, B_TILES, H], F32)
+
+        label_words = keep.tile([P, B_TILES * D // 2], I32)
+        nc.sync.dma_start(
+            out=label_words[:], in_=labels.bitcast(I32).rearrange("(p t) w -> p (t w)", t=B_TILES)
+        )
+
+        nc.vector.memset(rows[:, 0, :].bitcast(I32), 0)
+        for block in range(1, D + 1):
+            nc.gpsimd.memset(rows[:, block, :].bitcast(F32), 0.0)
+        for d in range(D):
+            nc.scalar.dma_start(out=rows[d : d + 1, d, :], in_=w1[d : d + 1, :])
+            nc.scalar.dma_start(out=rows[ROW_ONE : ROW_ONE + 1, d, :], in_=b1[d : d + 1, :])
+        nc.scalar.dma_start(out=rows[ROW_MISSING : ROW_MISSING + D, D, :], in_=emb_w)
+
+        nc.vector.memset(w_planes[:].rearrange("p d n -> p (d n)").bitcast(I32), 0)
+        for d in range(D):
+            for quadrant in range(4):
+                nc.sync.dma_start(
+                    out=w_planes[32 * quadrant : 32 * quadrant + 16, d, :].bitcast(I32),
+                    in_=w2_scales[
+                        PASSES * d : PASSES * (d + 1), 4 * quadrant : 4 * quadrant + 4, :
+                    ].bitcast(I32),
+                )
+        for g in range(D * PASSES):
+            nc.sync.dma_start(
+                out=w_words[:, g, :].bitcast(I32),
+                in_=w2_words[g].rearrange("p n t -> p (n t)").bitcast(I32),
+            )
+
+        identity = keep.tile([P, P], F32)
+        make_identity(nc, identity[:])
+        identity_bf = keep.tile([P, P], BF16)
+        nc.vector.tensor_copy(out=identity_bf[:], in_=identity[:])
+
+        label_bits = keep.tile([P, B_TILES * D], I32)
+        bit_pairs = label_bits[:].rearrange("p (w i) -> p w i", i=2)
+        nc.vector.tensor_single_scalar(
+            out=bit_pairs[:, :, 0], in_=label_words[:], scalar=16, op=ALU.logical_shift_left
+        )
+        nc.vector.tensor_single_scalar(
+            out=bit_pairs[:, :, 1], in_=label_words[:], scalar=-65536, op=ALU.bitwise_and
+        )
+        magnitude = keep.tile([P, B_TILES * D], I32)
+        nc.vector.tensor_single_scalar(
+            out=magnitude[:], in_=label_bits[:], scalar=0x7FFFFFFF, op=ALU.bitwise_and
+        )
+        present = keep.tile([P, B_TILES * D], F32)
+        nc.vector.tensor_single_scalar(
+            out=present[:], in_=magnitude[:], scalar=float(INFINITY_BITS), op=ALU.is_le
+        )
+        all_ones = keep.tile([P, B_TILES * D], I32)
+        nc.vector.tensor_scalar(
+            out=all_ones[:],
+            in0=magnitude[:],
+            scalar1=float(INFINITY_BITS),
+            scalar2=-1.0,
+            op0=ALU.is_le,
+            op1=ALU.mult,
+        )
+        safe_bits = keep.tile([P, B_TILES * D], I32)
+        nc.vector.tensor_tensor(
+            out=safe_bits[:], in0=label_bits[:], in1=all_ones[:], op=ALU.bitwise_and
+        )
+
+        def by_tile(ap):
+            return ap.rearrange("p (t d) -> p t d", t=B_TILES)
+
+        columns = keep.tile([P, B_TILES, P], BF16)
+        nc.vector.memset(columns[:].rearrange("p t k -> p (t k)").bitcast(I32), 0)
+        nc.vector.tensor_copy(out=columns[:, :, 0:D], in_=by_tile(safe_bits[:].bitcast(F32)))
+        nc.vector.memset(columns[:, :, ROW_ONE : ROW_ONE + 1], 1.0)
+        nc.vector.tensor_scalar(
+            out=columns[:, :, ROW_MISSING : ROW_MISSING + D],
+            in0=by_tile(present[:]),
+            scalar1=-1.0,
+            scalar2=1.0,
+            op0=ALU.mult,
+            op1=ALU.add,
+        )
+        columns_t = tr_pool.tile([P, B_TILES, P], BF16, tag="tr")
+        for t in range(B_TILES):
+            nc.tensor.transpose(columns_t[:, t, :], columns[:, t, :], identity_bf[:])
+        sample_rows = keep.tile([P, B_TILES, P], BF16)
+        nc.vector.tensor_copy(out=sample_rows[:], in_=columns_t[:])
+
+        e_tiles, max_tiles, sum_tiles, s_tiles = {}, {}, {}, {}
+
+        def logits(u, c):
+            d, t = UNITS[u]
+            if c == 0:
+                e_tiles[u] = work.tile([P, F], F32, name="e")
+                max_tiles[u] = small.tile([P, PASSES], F32, name="run_max")
+            run = slice(c * K_PASS, (c + 1) * K_PASS)
+            h1 = h1_pool.tile([P, K_PASS], F32)
+            nc.tensor.matmul(
+                out=h1[:], lhsT=sample_rows[:, t, :], rhs=rows[:, d, run], start=True, stop=True
+            )
+            nc.vector.tensor_scalar(
+                out=e_tiles[u][:, run].rearrange("b (u p i) -> b u p i", u=2, i=2),
+                in0=h1[:].rearrange("b (p u i) -> b u p i", u=2, i=2),
+                scalar1=1.0,
+                scalar2=None,
+                op0=ALU.mult,
+                op1=ALU.max,
+                accum_out=max_tiles[u][:, c : c + 1],
+            )
+
+        def row_maximum(u):
+            minus_max = small.tile([P, 1], F32)
+            nc.vector.tensor_reduce(
+                out=minus_max[:],
+                in_=max_tiles[u][:],
+                axis=mybir.AxisListType.X,
+                op=ALU.max,
+                negate=True,
+            )
+            max_tiles[u] = minus_max
+
+        def exponentials(u):
+            sum_tiles[u] = small.tile([P, 1], F32, name="total")
+            nc.scalar.activation(
+                out=e_tiles[u][:],
+                in_=e_tiles[u][:],
+                func=ACT.Exp,
+                bias=max_tiles[u][:],
+                scale=1.0,
+                accum_out=sum_tiles[u][:],
+            )
+
+        def normalise(u):
+            d, t = UNITS[u]
+            factor = small.tile([P, 1], F32)
+            nc.vector.reciprocal(out=factor[:], in_=sum_tiles[u][:])
+            column = t * D + d
+            nc.vector.tensor_mul(out=factor[:], in0=factor[:], in1=present[:, column : column + 1])
+            s_tiles[u] = work.tile([P, F], BF16, name="s")
+            nc.scalar.activation(out=s_tiles[u][:], in_=e_tiles[u][:], func=ACT.Copy, scale=factor[:])
+
+        def transpose_and_quantise(u):
+            d, t = UNITS[u]
+            grouped = work.tile([P, PASSES, P, 4], BF16, align_bytes=64)
+            grouped_pairs = (
+                grouped[:]
+                .rearrange("p c b j -> p (c b j)")
+                .bitcast(F32)
+                .rearrange("p (c b u) -> p c b u", c=PASSES, u=2)
+            )
+            s_pairs = s_tiles[u][:].bitcast(F32)
+            banks = [tr_pool.tile([P, 2, 2, P], F32, name="tr") for half in range(PASSES // 2)]
+            for c in range(PASSES):
+                for pair in range(2):
+                    first = (c * 2 + pair) * P
+                    nc.tensor.transpose(
+                        banks[c // 2][:, c % 2, pair, :], s_pairs[:, first : first + P], identity[:]
+                    )
+            for half in range(PASSES // 2):
+                nc.vector.tensor_copy(
+                    out=grouped_pairs[:, 2 * half : 2 * half + 2],
+                    in_=banks[half][:].rearrange("p c u b -> p c b u"),
+                )
+            passes = slice(PASSES * d, PASSES * (d + 1))
+            nc.vector.quantize_mx(
+                out=s_words[:, t, passes, :].rearrange("p g b -> p (g b)").bitcast(FP8X4),
+                scales=s_planes[:, t, passes, :].rearrange("p g b -> p (g b)"),
+                in_=grouped[:].rearrange("p c b j -> p (c b j)"),
+            )
+
+        acc = {}
+        out_rows = out.rearrange("(p t) n -> p t n", t=B_TILES)
+
+        def multiply(u, n):
+            d, t = UNITS[u]
+            cols = slice(n * N_TILE, (n + 1) * N_TILE)
+            if d == 0:
+                acc[n] = acc_pool.tile([P, N_TILE], F32, name="acc%d" % n)
+            for c in range(PASSES):
+                g = PASSES * d + c
+                nc.tensor.matmul_mx(
+                    out=acc[n][:],
+                    lhsT=s_words[:, t, g, :].bitcast(FP8X4),
+                    lhsT_scale=s_planes[:, t, g, :],
+                    rhs=w_words[:, g, cols].bitcast(FP8X4),
+                    rhs_scale=w_planes[4 * c : P, d, cols],
+                    start=(g == 0),
+                    stop=(g == D * PASSES - 1),
+                )
+            if d == D - 1:
+                nc.vector.tensor_tensor(
+                    out=result[:, t, cols], in0=acc[n][:], in1=result[:, t, cols], op=ALU.add
+                )
+                nc.sync.dma_start(out=out_rows[:, t, cols], in_=result[:, t, cols])
+
+        def missing_term():
+            for t in range(B_TILES):
+                for n in range(N_TILES):
+                    cols = slice(n * N_TILE, (n + 1) * N_TILE)
+                    emb = h1_pool.tile([P, N_TILE], F32, tag="h1")
+                    nc.tensor.matmul(
+                        out=emb[:],
+                        lhsT=sample_rows[:, t, :],
+                        rhs=rows[:, D, cols],
+                        start=True,
+                        stop=True,
+                    )
+                    nc.scalar.copy(out=result[:, t, cols], in_=emb[:])
+
+        def valid(u):
+            return 0 <= u < len(UNITS)
+
+        with tc.manual_schedule():
+            for i in range(-2, len(UNITS) + 1):
+                if valid(i + 1):
+                    exponentials(i + 1)
+                if valid(i):
+                    transpose_and_quantise(i)
+                for n in range(N_TILES):
+                    if valid(i + 2):
+                        logits(i + 2, n)
+                    if valid(i - 1):
+                        multiply(i - 1, n)
+                    if n == 0 and valid(i + 1):
+                        normalise(i + 1)
+                if valid(i + 2):
+                    row_maximum(i + 2)
+                if i == 0:
+                    missing_term()

@@ -50,6 +50,15 @@ def tile_conditionembedder_w_e_kernel(
         s_planes = keep.tile([P, B_TILES, D * PASSES, P], U8, align_bytes=64)
         result = keep.tile([P, B_TILES, H], F32)
 
+        identity = keep.tile([P, P], F32)
+        make_identity(nc, identity[:])
+        identity_bf = keep.tile([P, P], BF16)
+        nc.vector.tensor_copy(out=identity_bf[:], in_=identity[:])
+
+        warm = keep.tile([P, 1], F32)
+        nc.vector.memset(warm[:], 0.0)
+        nc.scalar.activation(out=warm[:], in_=warm[:], func=ACT.Exp)
+
         label_words = keep.tile([P, B_TILES * D // 2], I32)
         nc.sync.dma_start(
             out=label_words[:], in_=labels.bitcast(I32).rearrange("(p t) w -> p (t w)", t=B_TILES)
@@ -72,16 +81,11 @@ def tile_conditionembedder_w_e_kernel(
                         PASSES * d : PASSES * (d + 1), 4 * quadrant : 4 * quadrant + 4, :
                     ].bitcast(I32),
                 )
-        for g in range(D * PASSES):
-            nc.sync.dma_start(
-                out=w_words[:, g, :].bitcast(I32),
-                in_=w2_words[g].rearrange("p n t -> p (n t)").bitcast(I32),
-            )
-
-        identity = keep.tile([P, P], F32)
-        make_identity(nc, identity[:])
-        identity_bf = keep.tile([P, P], BF16)
-        nc.vector.tensor_copy(out=identity_bf[:], in_=identity[:])
+            for g in range(PASSES * d, PASSES * (d + 1)):
+                nc.sync.dma_start(
+                    out=w_words[:, g, :].bitcast(I32),
+                    in_=w2_words[g].rearrange("p n t -> p (n t)").bitcast(I32),
+                )
 
         label_bits = keep.tile([P, B_TILES * D], I32)
         bit_pairs = label_bits[:].rearrange("p (w i) -> p w i", i=2)
@@ -185,7 +189,7 @@ def tile_conditionembedder_w_e_kernel(
             column = t * D + d
             nc.vector.tensor_mul(out=factor[:], in0=factor[:], in1=present[:, column : column + 1])
             s_tiles[u] = work.tile([P, F], BF16, name="s")
-            nc.scalar.activation(out=s_tiles[u][:], in_=e_tiles[u][:], func=ACT.Copy, scale=factor[:])
+            nc.vector.tensor_scalar_mul(out=s_tiles[u][:], in0=e_tiles[u][:], scalar1=factor[:])
 
         def transpose_and_quantise(u):
             d, t = UNITS[u]
@@ -205,7 +209,7 @@ def tile_conditionembedder_w_e_kernel(
                         banks[c // 2][:, c % 2, pair, :], s_pairs[:, first : first + P], identity[:]
                     )
             for half in range(PASSES // 2):
-                nc.vector.tensor_copy(
+                nc.scalar.copy(
                     out=grouped_pairs[:, 2 * half : 2 * half + 2],
                     in_=banks[half][:].rearrange("p c u b -> p c b u"),
                 )
@@ -241,37 +245,32 @@ def tile_conditionembedder_w_e_kernel(
                 )
                 nc.sync.dma_start(out=out_rows[:, t, cols], in_=result[:, t, cols])
 
-        def missing_term():
-            for t in range(B_TILES):
-                for n in range(N_TILES):
-                    cols = slice(n * N_TILE, (n + 1) * N_TILE)
-                    emb = h1_pool.tile([P, N_TILE], F32, tag="h1")
-                    nc.tensor.matmul(
-                        out=emb[:],
-                        lhsT=sample_rows[:, t, :],
-                        rhs=rows[:, D, cols],
-                        start=True,
-                        stop=True,
-                    )
-                    nc.scalar.copy(out=result[:, t, cols], in_=emb[:])
+        def missing_term(t):
+            for n in range(N_TILES):
+                cols = slice(n * N_TILE, (n + 1) * N_TILE)
+                emb = h1_pool.tile([P, N_TILE], F32, tag="h1")
+                nc.tensor.matmul(
+                    out=emb[:], lhsT=sample_rows[:, t, :], rhs=rows[:, D, cols], start=True, stop=True
+                )
+                nc.scalar.copy(out=result[:, t, cols], in_=emb[:])
 
         def valid(u):
             return 0 <= u < len(UNITS)
 
         with tc.manual_schedule():
-            for i in range(-2, len(UNITS) + 1):
-                if valid(i + 1):
-                    exponentials(i + 1)
-                if valid(i):
-                    transpose_and_quantise(i)
+            for i in range(-3, len(UNITS)):
                 for n in range(N_TILES):
-                    if valid(i + 2):
-                        logits(i + 2, n)
-                    if valid(i - 1):
-                        multiply(i - 1, n)
-                    if n == 0 and valid(i + 1):
-                        normalise(i + 1)
+                    if n == 2 and valid(i + 1):
+                        transpose_and_quantise(i + 1)
+                    if n == 3 and valid(i + 2):
+                        exponentials(i + 2)
+                    if valid(i + 3):
+                        logits(i + 3, n)
+                    if valid(i):
+                        multiply(i, n)
+                if valid(i + 3):
+                    row_maximum(i + 3)
                 if valid(i + 2):
-                    row_maximum(i + 2)
-                if i == 0:
-                    missing_term()
+                    normalise(i + 2)
+                if valid(i + 2) and UNITS[i + 2][0] == 0:
+                    missing_term(UNITS[i + 2][1])

@@ -21,10 +21,16 @@ N_TILE = 512
 N_TILES = H // N_TILE
 INFINITY_BITS = 0x7F800000
 
-ROW_ONE = D
-ROW_MISSING = D + 1
+ROW_B1 = D
+ROW_EMB = 2 * D
 
-UNITS = [(d, t) for t in range(B_TILES) for d in range(D)]
+PARTS = (((0, 0), (1, 0)), ((0, 1), (1, 1), (2, 1), (3, 1)), ((2, 0), (3, 0)))
+UNITS = [unit for part in PARTS for unit in part]
+OPENS = [sum(len(q) for q in PARTS[:i]) for i in range(len(PARTS))]
+CLOSES = [sum(len(q) for q in PARTS[: i + 1]) - 1 for i in range(len(PARTS))]
+STORES = [CLOSES[1], CLOSES[2]]
+PER_TICK = PASSES * N_TILES
+M1, M2, M3 = 5, 2, 3
 
 FLOPS = 2 * B * D * F * H
 
@@ -42,35 +48,32 @@ def tile_conditionembedder_w_e_kernel(
         acc_pool = ctx.enter_context(tc.psum_pool(name="acc", bufs=1))
         h1_pool = ctx.enter_context(tc.psum_pool(name="h1", bufs=2))
         tr_pool = ctx.enter_context(tc.psum_pool(name="tr", bufs=2))
+        ctx.enter_context(tc.manual_schedule())
 
-        rows = keep.tile([P, D + 1, F], BF16)
+        rows = keep.tile([P, F], BF16)
         w_words = keep.tile([P, D * PASSES, H], U32, align_bytes=64)
         w_planes = keep.tile([P, D, H], U8, align_bytes=64)
         s_words = keep.tile([P, B_TILES, D * PASSES, P], U32, align_bytes=64)
         s_planes = keep.tile([P, B_TILES, D * PASSES, P], U8, align_bytes=64)
         result = keep.tile([P, B_TILES, H], F32)
-
         identity = keep.tile([P, P], F32)
-        make_identity(nc, identity[:])
         identity_bf = keep.tile([P, P], BF16)
-        nc.vector.tensor_copy(out=identity_bf[:], in_=identity[:])
-
         warm = keep.tile([P, 1], F32)
-        nc.vector.memset(warm[:], 0.0)
-        nc.scalar.activation(out=warm[:], in_=warm[:], func=ACT.Exp)
-
         label_words = keep.tile([P, B_TILES * D // 2], I32)
+        columns = keep.tile([P, B_TILES, P], BF16)
+        selectors = keep.tile([P, D + 1], F32)
+        sample_rows = keep.tile([P, D + 1, B_TILES, P], BF16)
+
         nc.sync.dma_start(
             out=label_words[:], in_=labels.bitcast(I32).rearrange("(p t) w -> p (t w)", t=B_TILES)
         )
-
-        nc.vector.memset(rows[:, 0, :].bitcast(I32), 0)
-        for block in range(1, D + 1):
-            nc.gpsimd.memset(rows[:, block, :].bitcast(F32), 0.0)
-        for d in range(D):
-            nc.scalar.dma_start(out=rows[d : d + 1, d, :], in_=w1[d : d + 1, :])
-            nc.scalar.dma_start(out=rows[ROW_ONE : ROW_ONE + 1, d, :], in_=b1[d : d + 1, :])
-        nc.scalar.dma_start(out=rows[ROW_MISSING : ROW_MISSING + D, D, :], in_=emb_w)
+        make_identity(nc, identity[:])
+        nc.vector.memset(rows[:].bitcast(I32), 0)
+        nc.scalar.dma_start(out=rows[0:D, :], in_=w1)
+        nc.scalar.dma_start(out=rows[ROW_B1 : ROW_B1 + D, :], in_=b1)
+        nc.scalar.dma_start(out=rows[ROW_EMB : ROW_EMB + D, :], in_=emb_w)
+        nc.vector.memset(warm[:], 0.0)
+        nc.scalar.activation(out=warm[:], in_=warm[:], func=ACT.Exp)
 
         nc.vector.memset(w_planes[:].rearrange("p d n -> p (d n)").bitcast(I32), 0)
         for d in range(D):
@@ -87,6 +90,19 @@ def tile_conditionembedder_w_e_kernel(
                     in_=w2_words[g].rearrange("p n t -> p (n t)").bitcast(I32),
                 )
 
+        nc.vector.memset(columns[:].rearrange("p t k -> p (t k)").bitcast(I32), 0)
+        nc.vector.memset(columns[:, :, ROW_B1 : ROW_B1 + D], 1.0)
+        nc.vector.tensor_copy(out=identity_bf[:], in_=identity[:])
+        nc.vector.tensor_tensor(
+            out=selectors[:, 0:D], in0=identity[:, 0:D], in1=identity[:, ROW_B1 : ROW_B1 + D], op=ALU.add
+        )
+        nc.vector.tensor_reduce(
+            out=selectors[:, D : D + 1],
+            in_=identity[:, ROW_EMB : ROW_EMB + D],
+            axis=mybir.AxisListType.X,
+            op=ALU.add,
+        )
+
         label_bits = keep.tile([P, B_TILES * D], I32)
         bit_pairs = label_bits[:].rearrange("p (w i) -> p w i", i=2)
         nc.vector.tensor_single_scalar(
@@ -98,10 +114,6 @@ def tile_conditionembedder_w_e_kernel(
         magnitude = keep.tile([P, B_TILES * D], I32)
         nc.vector.tensor_single_scalar(
             out=magnitude[:], in_=label_bits[:], scalar=0x7FFFFFFF, op=ALU.bitwise_and
-        )
-        present = keep.tile([P, B_TILES * D], F32)
-        nc.vector.tensor_single_scalar(
-            out=present[:], in_=magnitude[:], scalar=float(INFINITY_BITS), op=ALU.is_le
         )
         all_ones = keep.tile([P, B_TILES * D], I32)
         nc.vector.tensor_scalar(
@@ -120,12 +132,13 @@ def tile_conditionembedder_w_e_kernel(
         def by_tile(ap):
             return ap.rearrange("p (t d) -> p t d", t=B_TILES)
 
-        columns = keep.tile([P, B_TILES, P], BF16)
-        nc.vector.memset(columns[:].rearrange("p t k -> p (t k)").bitcast(I32), 0)
         nc.vector.tensor_copy(out=columns[:, :, 0:D], in_=by_tile(safe_bits[:].bitcast(F32)))
-        nc.vector.memset(columns[:, :, ROW_ONE : ROW_ONE + 1], 1.0)
+        present = keep.tile([P, B_TILES * D], F32)
+        nc.vector.tensor_single_scalar(
+            out=present[:], in_=magnitude[:], scalar=float(INFINITY_BITS), op=ALU.is_le
+        )
         nc.vector.tensor_scalar(
-            out=columns[:, :, ROW_MISSING : ROW_MISSING + D],
+            out=columns[:, :, ROW_EMB : ROW_EMB + D],
             in0=by_tile(present[:]),
             scalar1=-1.0,
             scalar2=1.0,
@@ -135,21 +148,32 @@ def tile_conditionembedder_w_e_kernel(
         columns_t = tr_pool.tile([P, B_TILES, P], BF16, tag="tr")
         for t in range(B_TILES):
             nc.tensor.transpose(columns_t[:, t, :], columns[:, t, :], identity_bf[:])
-        sample_rows = keep.tile([P, B_TILES, P], BF16)
-        nc.vector.tensor_copy(out=sample_rows[:], in_=columns_t[:])
 
-        e_tiles, max_tiles, sum_tiles, s_tiles = {}, {}, {}, {}
+        def stationary(v):
+            nc.vector.tensor_scalar_mul(
+                out=sample_rows[:, v, :, :].rearrange("k t b -> k (t b)"),
+                in0=columns_t[:].rearrange("k t b -> k (t b)"),
+                scalar1=selectors[:, v : v + 1],
+            )
+
+        stationary(0)
+
+        e_tiles, max_tiles, sum_tiles, s_tiles, factors, grouped_tiles, banks, h1_tiles = {}, {}, {}, {}, {}, {}, {}, {}
 
         def logits(u, c):
             d, t = UNITS[u]
+            run = slice(c * K_PASS, (c + 1) * K_PASS)
+            h1_tiles[(u, c)] = h1_pool.tile([P, K_PASS], F32, name="h1")
+            nc.tensor.matmul(
+                out=h1_tiles[(u, c)][:], lhsT=sample_rows[:, d, t, :], rhs=rows[:, run], start=True, stop=True
+            )
+
+        def evacuate(u, c):
             if c == 0:
                 e_tiles[u] = work.tile([P, F], F32, name="e")
                 max_tiles[u] = small.tile([P, PASSES], F32, name="run_max")
             run = slice(c * K_PASS, (c + 1) * K_PASS)
-            h1 = h1_pool.tile([P, K_PASS], F32)
-            nc.tensor.matmul(
-                out=h1[:], lhsT=sample_rows[:, t, :], rhs=rows[:, d, run], start=True, stop=True
-            )
+            h1 = h1_tiles[(u, c)]
             nc.vector.tensor_scalar(
                 out=e_tiles[u][:, run].rearrange("b (u p i) -> b u p i", u=2, i=2),
                 in0=h1[:].rearrange("b (p u i) -> b u p i", u=2, i=2),
@@ -182,95 +206,181 @@ def tile_conditionembedder_w_e_kernel(
                 accum_out=sum_tiles[u][:],
             )
 
-        def normalise(u):
+        def normalise(u, first, last):
             d, t = UNITS[u]
-            factor = small.tile([P, 1], F32)
-            nc.vector.reciprocal(out=factor[:], in_=sum_tiles[u][:])
-            column = t * D + d
-            nc.vector.tensor_mul(out=factor[:], in0=factor[:], in1=present[:, column : column + 1])
-            s_tiles[u] = work.tile([P, F], BF16, name="s")
-            nc.vector.tensor_scalar_mul(out=s_tiles[u][:], in0=e_tiles[u][:], scalar1=factor[:])
+            if first == 0:
+                factor = small.tile([P, 1], F32)
+                nc.vector.reciprocal(out=factor[:], in_=sum_tiles[u][:])
+                column = t * D + d
+                nc.vector.tensor_mul(out=factor[:], in0=factor[:], in1=present[:, column : column + 1])
+                factors[u] = factor
+                s_tiles[u] = work.tile([P, F], BF16, name="s")
+            cols = slice(first * K_PASS, last * K_PASS)
+            nc.vector.tensor_scalar_mul(
+                out=s_tiles[u][:, cols], in0=e_tiles[u][:, cols], scalar1=factors[u][:]
+            )
 
-        def transpose_and_quantise(u):
-            d, t = UNITS[u]
-            grouped = work.tile([P, PASSES, P, 4], BF16, align_bytes=64)
+        def transposes(u, first, last):
+            s_pairs = s_tiles[u][:].bitcast(F32)
+            for c in range(first, last):
+                if (c - first) % 2 == 0:
+                    banks[(u, c)] = tr_pool.tile([P, 2, 2, P], F32, name="tr")
+                else:
+                    banks[(u, c)] = banks[(u, c - 1)]
+                for pair in range(2):
+                    begin = (c * 2 + pair) * P
+                    nc.tensor.transpose(
+                        banks[(u, c)][:, (c - first) % 2, pair, :], s_pairs[:, begin : begin + P], identity[:]
+                    )
+
+        def copies(u, first, last):
+            if first == 0:
+                grouped_tiles[u] = work.tile([P, PASSES, P, 4], BF16, name="grouped", align_bytes=64)
             grouped_pairs = (
-                grouped[:]
+                grouped_tiles[u][:]
                 .rearrange("p c b j -> p (c b j)")
                 .bitcast(F32)
                 .rearrange("p (c b u) -> p c b u", c=PASSES, u=2)
             )
-            s_pairs = s_tiles[u][:].bitcast(F32)
-            banks = [tr_pool.tile([P, 2, 2, P], F32, name="tr") for half in range(PASSES // 2)]
-            for c in range(PASSES):
-                for pair in range(2):
-                    first = (c * 2 + pair) * P
-                    nc.tensor.transpose(
-                        banks[c // 2][:, c % 2, pair, :], s_pairs[:, first : first + P], identity[:]
-                    )
-            for half in range(PASSES // 2):
+            for c in range(first, last, 2):
+                count = min(2, last - c)
                 nc.scalar.copy(
-                    out=grouped_pairs[:, 2 * half : 2 * half + 2],
-                    in_=banks[half][:].rearrange("p c u b -> p c b u"),
+                    out=grouped_pairs[:, c : c + count],
+                    in_=banks[(u, c)][:, 0:count].rearrange("p c u b -> p c b u"),
                 )
-            passes = slice(PASSES * d, PASSES * (d + 1))
+
+        quantised = set()
+
+        def quantise(u, first, last):
+            d, t = UNITS[u]
+            passes = slice(PASSES * d + first, PASSES * d + last)
             nc.vector.quantize_mx(
                 out=s_words[:, t, passes, :].rearrange("p g b -> p (g b)").bitcast(FP8X4),
                 scales=s_planes[:, t, passes, :].rearrange("p g b -> p (g b)"),
-                in_=grouped[:].rearrange("p c b j -> p (c b j)"),
+                in_=grouped_tiles[u][:, first:last].rearrange("p c b j -> p (c b j)"),
             )
+            for c in range(first, last):
+                quantised.add((u, c))
 
         acc = {}
         out_rows = out.rearrange("(p t) n -> p t n", t=B_TILES)
 
-        def multiply(u, n):
+        def one_pass(u, c, n):
             d, t = UNITS[u]
+            g = PASSES * d + c
             cols = slice(n * N_TILE, (n + 1) * N_TILE)
-            if d == 0:
+            first = u in OPENS and c == 0
+            last = u in CLOSES and c == PASSES - 1
+            if first:
                 acc[n] = acc_pool.tile([P, N_TILE], F32, name="acc%d" % n)
-            for c in range(PASSES):
-                g = PASSES * d + c
-                nc.tensor.matmul_mx(
-                    out=acc[n][:],
-                    lhsT=s_words[:, t, g, :].bitcast(FP8X4),
-                    lhsT_scale=s_planes[:, t, g, :],
-                    rhs=w_words[:, g, cols].bitcast(FP8X4),
-                    rhs_scale=w_planes[4 * c : P, d, cols],
-                    start=(g == 0),
-                    stop=(g == D * PASSES - 1),
-                )
-            if d == D - 1:
+            nc.tensor.matmul_mx(
+                out=acc[n][:],
+                lhsT=s_words[:, t, g, :].bitcast(FP8X4),
+                lhsT_scale=s_planes[:, t, g, :],
+                rhs=w_words[:, g, cols].bitcast(FP8X4),
+                rhs_scale=w_planes[4 * c : P, d, cols],
+                start=first,
+                stop=last,
+            )
+            if last:
                 nc.vector.tensor_tensor(
                     out=result[:, t, cols], in0=acc[n][:], in1=result[:, t, cols], op=ALU.add
                 )
-                nc.sync.dma_start(out=out_rows[:, t, cols], in_=result[:, t, cols])
+                if u in STORES:
+                    nc.sync.dma_start(out=out_rows[:, t, cols], in_=result[:, t, cols])
 
-        def missing_term(t):
-            for n in range(N_TILES):
-                cols = slice(n * N_TILE, (n + 1) * N_TILE)
-                emb = h1_pool.tile([P, N_TILE], F32, tag="h1")
-                nc.tensor.matmul(
-                    out=emb[:], lhsT=sample_rows[:, t, :], rhs=rows[:, D, cols], start=True, stop=True
-                )
-                nc.scalar.copy(out=result[:, t, cols], in_=emb[:])
+        pending = []
+        for u in range(len(UNITS)):
+            if u in CLOSES:
+                pending.extend((u, c, n) for c in range(2) for n in range(N_TILES))
+                pending.extend((u, c, n) for n in range(N_TILES) for c in range(2, PASSES))
+            else:
+                pending.extend((u, c, n) for c in range(PASSES) for n in range(N_TILES))
+        done = []
+
+        def multiply(count):
+            for k in range(count):
+                if len(done) == len(pending) or pending[len(done)][0:2] not in quantised:
+                    return
+                one_pass(*pending[len(done)])
+                done.append(1)
+
+        def missing_term(t, n, pool_tile):
+            cols = slice(n * N_TILE, (n + 1) * N_TILE)
+            nc.tensor.matmul(
+                out=pool_tile[:], lhsT=sample_rows[:, D, t, :], rhs=rows[:, cols], start=True, stop=True
+            )
+            return cols
 
         def valid(u):
             return 0 <= u < len(UNITS)
 
-        with tc.manual_schedule():
-            for i in range(-3, len(UNITS)):
-                for n in range(N_TILES):
-                    if n == 2 and valid(i + 1):
-                        transpose_and_quantise(i + 1)
-                    if n == 3 and valid(i + 2):
-                        exponentials(i + 2)
-                    if valid(i + 3):
-                        logits(i + 3, n)
-                    if valid(i):
-                        multiply(i, n)
-                if valid(i + 3):
-                    row_maximum(i + 3)
-                if valid(i + 2):
-                    normalise(i + 2)
-                if valid(i + 2) and UNITS[i + 2][0] == 0:
-                    missing_term(UNITS[i + 2][1])
+        def valid_tile(n):
+            return 0 <= n < N_TILES
+
+        def missing_tile(t, n, bank):
+            cols = missing_term(t, n, bank)
+            nc.scalar.copy(out=result[:, t, cols], in_=bank[:])
+
+        def head_bank(n):
+            return acc_pool.tile([P, N_TILE], F32, name="acc%d" % n)
+
+        stationary(D)
+        logits(0, 0)
+        logits(0, 1)
+        evacuate(0, 0)
+        evacuate(0, 1)
+        missing_tile(0, 0, head_bank(0))
+        logits(0, 2)
+        missing_tile(0, 1, head_bank(1))
+        logits(0, 3)
+        missing_tile(0, 2, head_bank(2))
+        missing_tile(0, 3, head_bank(3))
+        evacuate(0, 2)
+        evacuate(0, 3)
+        row_maximum(0)
+        exponentials(0)
+        for v in range(1, D):
+            stationary(v)
+        for c in range(PASSES):
+            logits(1, c)
+            evacuate(1, c)
+        row_maximum(1)
+        logits(2, 0)
+        logits(2, 1)
+        for c in range(PASSES):
+            normalise(0, c, c + 1)
+            transposes(0, c, c + 1)
+            copies(0, c, c + 1)
+        exponentials(1)
+        for c in range(PASSES):
+            quantise(0, c, c + 1)
+
+        for a in range(2, len(UNITS) + 1):
+            if valid(a):
+                evacuate(a, 0)
+                evacuate(a, 1)
+            multiply(M1)
+            if valid_tile(a - 2):
+                missing_tile(1, a - 2, h1_pool.tile([P, N_TILE], F32, name="h1"))
+            if valid(a):
+                logits(a, 2)
+            multiply(M2)
+            if valid(a):
+                logits(a, 3)
+            normalise(a - 1, 0, PASSES)
+            if valid(a):
+                evacuate(a, 2)
+                evacuate(a, 3)
+                row_maximum(a)
+            multiply(M3)
+            transposes(a - 1, 0, PASSES)
+            copies(a - 1, 0, PASSES)
+            if valid(a):
+                exponentials(a)
+            quantise(a - 1, 0, PASSES)
+            multiply(PER_TICK - M1 - M2 - M3)
+            if valid(a + 1):
+                logits(a + 1, 0)
+                logits(a + 1, 1)
+        multiply(len(pending))

@@ -84,11 +84,11 @@ def tile_conditionembedder_w_e_kernel(
                         PASSES * d : PASSES * (d + 1), 4 * quadrant : 4 * quadrant + 4, :
                     ].bitcast(I32),
                 )
-            for g in range(PASSES * d, PASSES * (d + 1)):
-                nc.sync.dma_start(
-                    out=w_words[:, g, :].bitcast(I32),
-                    in_=w2_words[g].rearrange("p n t -> p (n t)").bitcast(I32),
-                )
+        for g in range(D * PASSES):
+            nc.sync.dma_start(
+                out=w_words[:, g, :].bitcast(I32),
+                in_=w2_words[g].rearrange("p n t -> p (n t)").bitcast(I32),
+            )
 
         nc.vector.memset(columns[:].rearrange("p t k -> p (t k)").bitcast(I32), 0)
         nc.vector.memset(columns[:, :, ROW_B1 : ROW_B1 + D], 1.0)

@@ -31,6 +31,7 @@ CLOSES = [sum(len(q) for q in PARTS[: i + 1]) - 1 for i in range(len(PARTS))]
 STORES = [CLOSES[1], CLOSES[2]]
 PER_TICK = PASSES * N_TILES
 M1, M2, M3 = 5, 2, 3
+HEAD_TILES = 2
 
 FLOPS = 2 * B * D * F * H
 
@@ -348,6 +349,8 @@ def tile_conditionembedder_w_e_kernel(
         row_maximum(1)
         logits(2, 0)
         logits(2, 1)
+        for n in range(HEAD_TILES):
+            missing_tile(1, n, head_bank(n))
         for c in range(PASSES):
             normalise(0, c, c + 1)
             transposes(0, c, c + 1)
@@ -361,8 +364,8 @@ def tile_conditionembedder_w_e_kernel(
                 evacuate(a, 0)
                 evacuate(a, 1)
             multiply(M1)
-            if valid_tile(a - 2):
-                missing_tile(1, a - 2, h1_pool.tile([P, N_TILE], F32, name="h1"))
+            if valid_tile(a - 2 + HEAD_TILES):
+                missing_tile(1, a - 2 + HEAD_TILES, h1_pool.tile([P, N_TILE], F32, name="h1"))
             if valid(a):
                 logits(a, 2)
             multiply(M2)

@@ -30,7 +30,7 @@ OPENS = [sum(len(q) for q in PARTS[:i]) for i in range(len(PARTS))]
 CLOSES = [sum(len(q) for q in PARTS[: i + 1]) - 1 for i in range(len(PARTS))]
 STORES = [CLOSES[1], CLOSES[2]]
 PER_TICK = PASSES * N_TILES
-M1, M2, M3 = 5, 2, 3
+BEFORE = 10
 HEAD_TILES = 2
 
 FLOPS = 2 * B * D * F * H
@@ -363,26 +363,22 @@ def tile_conditionembedder_w_e_kernel(
             if valid(a):
                 evacuate(a, 0)
                 evacuate(a, 1)
-            multiply(M1)
+            normalise(a - 1, 0, PASSES)
+            multiply(BEFORE)
             if valid_tile(a - 2 + HEAD_TILES):
                 missing_tile(1, a - 2 + HEAD_TILES, h1_pool.tile([P, N_TILE], F32, name="h1"))
             if valid(a):
                 logits(a, 2)
-            multiply(M2)
-            if valid(a):
                 logits(a, 3)
-            normalise(a - 1, 0, PASSES)
+            transposes(a - 1, 0, PASSES)
+            copies(a - 1, 0, PASSES)
             if valid(a):
                 evacuate(a, 2)
                 evacuate(a, 3)
                 row_maximum(a)
-            multiply(M3)
-            transposes(a - 1, 0, PASSES)
-            copies(a - 1, 0, PASSES)
-            if valid(a):
                 exponentials(a)
             quantise(a - 1, 0, PASSES)
-            multiply(PER_TICK - M1 - M2 - M3)
+            multiply(PER_TICK - BEFORE)
             if valid(a + 1):
                 logits(a + 1, 0)
                 logits(a + 1, 1)

@@ -31,7 +31,7 @@ CLOSES = [sum(len(q) for q in PARTS[: i + 1]) - 1 for i in range(len(PARTS))]
 STORES = [CLOSES[1], CLOSES[2]]
 PER_TICK = PASSES * N_TILES
 BEFORE = 10
-HEAD_TILES = 2
+HEAD_TILES = 4
 
 FLOPS = 2 * B * D * F * H
 

@@ -31,7 +31,6 @@ CLOSES = [sum(len(q) for q in PARTS[: i + 1]) - 1 for i in range(len(PARTS))]
 STORES = [CLOSES[1], CLOSES[2]]
 PER_TICK = PASSES * N_TILES
 BEFORE = 10
-HEAD_TILES = 4
 
 FLOPS = 2 * B * D * F * H
 
@@ -155,6 +154,14 @@ def tile_conditionembedder_w_e_kernel(
                 out=sample_rows[:, v, :, :].rearrange("k t b -> k (t b)"),
                 in0=columns_t[:].rearrange("k t b -> k (t b)"),
                 scalar1=selectors[:, v : v + 1],
+            )
+
+        def stationary_on_scalar(v):
+            nc.scalar.activation(
+                out=sample_rows[:, v, :, :].rearrange("k t b -> k (t b)"),
+                in_=columns_t[:].rearrange("k t b -> k (t b)"),
+                func=ACT.Copy,
+                scale=selectors[:, v : v + 1],
             )
 
         stationary(0)
@@ -292,7 +299,10 @@ def tile_conditionembedder_w_e_kernel(
 
         pending = []
         for u in range(len(UNITS)):
-            if u in CLOSES:
+            if u == 0:
+                pending.extend((u, c, n) for c in range(PASSES) for n in (0, 1))
+                pending.extend((u, c, n) for c in range(PASSES) for n in (2, 3))
+            elif u in CLOSES:
                 pending.extend((u, c, n) for c in range(2) for n in range(N_TILES))
                 pending.extend((u, c, n) for n in range(N_TILES) for c in range(2, PASSES))
             else:
@@ -316,57 +326,93 @@ def tile_conditionembedder_w_e_kernel(
         def valid(u):
             return 0 <= u < len(UNITS)
 
-        def valid_tile(n):
-            return 0 <= n < N_TILES
+        missing_banks = {}
 
-        def missing_tile(t, n, bank):
-            cols = missing_term(t, n, bank)
-            nc.scalar.copy(out=result[:, t, cols], in_=bank[:])
+        def missing_product(t, n):
+            missing_banks[(t, n)] = acc_pool.tile([P, N_TILE], F32, name="acc%d" % n)
+            missing_term(t, n, missing_banks[(t, n)])
 
-        def head_bank(n):
-            return acc_pool.tile([P, N_TILE], F32, name="acc%d" % n)
+        def missing_copy(t, n):
+            cols = slice(n * N_TILE, (n + 1) * N_TILE)
+            nc.scalar.copy(out=result[:, t, cols], in_=missing_banks[(t, n)][:])
 
         stationary(D)
+        for v in range(1, D):
+            stationary_on_scalar(v)
         logits(0, 0)
         logits(0, 1)
         evacuate(0, 0)
         evacuate(0, 1)
-        missing_tile(0, 0, head_bank(0))
+        missing_product(0, 0)
+        missing_copy(0, 0)
         logits(0, 2)
-        missing_tile(0, 1, head_bank(1))
+        missing_product(0, 1)
+        missing_copy(0, 1)
         logits(0, 3)
-        missing_tile(0, 2, head_bank(2))
-        missing_tile(0, 3, head_bank(3))
+        missing_product(0, 2)
+        missing_copy(0, 2)
+        missing_product(0, 3)
+        missing_copy(0, 3)
         evacuate(0, 2)
         evacuate(0, 3)
         row_maximum(0)
         exponentials(0)
-        for v in range(1, D):
-            stationary(v)
         for c in range(PASSES):
             logits(1, c)
             evacuate(1, c)
         row_maximum(1)
         logits(2, 0)
         logits(2, 1)
-        for n in range(HEAD_TILES):
-            missing_tile(1, n, head_bank(n))
-        for c in range(PASSES):
-            normalise(0, c, c + 1)
-            transposes(0, c, c + 1)
-            copies(0, c, c + 1)
+        for n in range(N_TILES):
+            missing_product(1, n)
+        missing_copy(1, 0)
+        missing_copy(1, 1)
+        normalise(0, 0, 1)
+        transposes(0, 0, 1)
+        copies(0, 0, 1)
+        normalise(0, 1, 2)
+        transposes(0, 1, 2)
+        copies(0, 1, 2)
         exponentials(1)
-        for c in range(PASSES):
-            quantise(0, c, c + 1)
+        normalise(0, 2, 3)
+        transposes(0, 2, 3)
+        quantise(0, 0, 1)
+        normalise(0, 3, 4)
+        transposes(0, 3, 4)
+        quantise(0, 1, 2)
+        multiply(4)
+        evacuate(2, 0)
+        evacuate(2, 1)
+        copies(0, 2, 3)
+        copies(0, 3, 4)
+        missing_copy(1, 2)
+        missing_copy(1, 3)
+        logits(2, 2)
+        logits(2, 3)
+        normalise(1, 0, 2)
+        quantise(0, 2, 3)
+        quantise(0, 3, 4)
+        normalise(1, 2, 4)
+        multiply(4)
+        transposes(1, 0, 2)
+        transposes(1, 2, 4)
+        copies(1, 0, 2)
+        copies(1, 2, 4)
+        multiply(8)
+        evacuate(2, 2)
+        evacuate(2, 3)
+        row_maximum(2)
+        exponentials(2)
+        quantise(1, 0, PASSES)
+        logits(3, 0)
+        logits(3, 1)
 
-        for a in range(2, len(UNITS) + 1):
+        for a in range(3, len(UNITS) + 1):
             if valid(a):
                 evacuate(a, 0)
                 evacuate(a, 1)
             normalise(a - 1, 0, PASSES)
             multiply(BEFORE)
-            if valid_tile(a - 2 + HEAD_TILES):
-                missing_tile(1, a - 2 + HEAD_TILES, h1_pool.tile([P, N_TILE], F32, name="h1"))
             if valid(a):
                 logits(a, 2)
                 logits(a, 3)

@@ -68,6 +68,7 @@ def tile_conditionembedder_w_e_kernel(
             out=label_words[:], in_=labels.bitcast(I32).rearrange("(p t) w -> p (t w)", t=B_TILES)
         )
         make_identity(nc, identity[:])
+        nc.vector.memset(w_planes[:, 0, :].bitcast(I32), 0)
         nc.vector.memset(rows[:].bitcast(I32), 0)
         nc.scalar.dma_start(out=rows[0:D, :], in_=w1)
         nc.scalar.dma_start(out=rows[ROW_B1 : ROW_B1 + D, :], in_=b1)
@@ -75,7 +76,7 @@ def tile_conditionembedder_w_e_kernel(
         nc.vector.memset(warm[:], 0.0)
         nc.scalar.activation(out=warm[:], in_=warm[:], func=ACT.Exp)
 
-        nc.vector.memset(w_planes[:].rearrange("p d n -> p (d n)").bitcast(I32), 0)
+        nc.vector.memset(w_planes[:, 1:D, :].rearrange("p d n -> p (d n)").bitcast(I32), 0)
         for d in range(D):
             for quadrant in range(4):
                 nc.sync.dma_start(
@@ -84,11 +85,11 @@ def tile_conditionembedder_w_e_kernel(
                         PASSES * d : PASSES * (d + 1), 4 * quadrant : 4 * quadrant + 4, :
                     ].bitcast(I32),
                 )
-        for g in range(D * PASSES):
-            nc.sync.dma_start(
-                out=w_words[:, g, :].bitcast(I32),
-                in_=w2_words[g].rearrange("p n t -> p (n t)").bitcast(I32),
-            )
+            for g in range(PASSES * d, PASSES * (d + 1)):
+                nc.sync.dma_start(
+                    out=w_words[:, g, :].bitcast(I32),
+                    in_=w2_words[g].rearrange("p n t -> p (n t)").bitcast(I32),
+                )
 
         nc.vector.memset(columns[:].rearrange("p t k -> p (t k)").bitcast(I32), 0)
         nc.vector.memset(columns[:, :, ROW_B1 : ROW_B1 + D], 1.0)
@@ -226,6 +227,12 @@ def tile_conditionembedder_w_e_kernel(
             cols = slice(first * K_PASS, last * K_PASS)
             nc.vector.tensor_scalar_mul(
                 out=s_tiles[u][:, cols], in0=e_tiles[u][:, cols], scalar1=factors[u][:]
+            )
+
+        def normalise_on_scalar(u, first, last):
+            cols = slice(first * K_PASS, last * K_PASS)
+            nc.scalar.activation(
+                out=s_tiles[u][:, cols], in_=e_tiles[u][:, cols], func=ACT.Copy, scale=factors[u][:]
             )
 
         def transposes(u, first, last):
@@ -411,7 +418,8 @@ def tile_conditionembedder_w_e_kernel(
             if valid(a):
                 evacuate(a, 0)
                 evacuate(a, 1)
-            normalise(a - 1, 0, PASSES)
+            normalise(a - 1, 0, 2)
+            normalise_on_scalar(a - 1, 2, PASSES)
             multiply(BEFORE)
             if valid(a):
                 logits(a, 2)

@@ -215,14 +215,18 @@ def tile_conditionembedder_w_e_kernel(
                 accum_out=sum_tiles[u][:],
             )
 
-        def normalise(u, first, last):
+        def make_factor(u):
             d, t = UNITS[u]
+            factor = small.tile([P, 1], F32)
+            nc.vector.reciprocal(out=factor[:], in_=sum_tiles[u][:])
+            column = t * D + d
+            nc.vector.tensor_mul(out=factor[:], in0=factor[:], in1=present[:, column : column + 1])
+            factors[u] = factor
+
+        def normalise(u, first, last):
             if first == 0:
-                factor = small.tile([P, 1], F32)
-                nc.vector.reciprocal(out=factor[:], in_=sum_tiles[u][:])
-                column = t * D + d
-                nc.vector.tensor_mul(out=factor[:], in0=factor[:], in1=present[:, column : column + 1])
-                factors[u] = factor
+                if u not in factors:
+                    make_factor(u)
                 s_tiles[u] = work.tile([P, F], BF16, name="s")
             cols = slice(first * K_PASS, last * K_PASS)
             nc.vector.tensor_scalar_mul(
@@ -383,9 +387,9 @@ def tile_conditionembedder_w_e_kernel(
         exponentials(1)
         normalise(0, 2, 3)
         transposes(0, 2, 3)
-        quantise(0, 0, 1)
         normalise(0, 3, 4)
         transposes(0, 3, 4)
+        quantise(0, 0, 1)
         quantise(0, 1, 2)
         multiply(4)
         evacuate(2, 0)
@@ -396,9 +400,10 @@ def tile_conditionembedder_w_e_kernel(
         missing_copy(1, 3)
         logits(2, 2)
         logits(2, 3)
-        normalise(1, 0, 2)
+        make_factor(1)
         quantise(0, 2, 3)
         quantise(0, 3, 4)
+        normalise(1, 0, 2)
         normalise(1, 2, 4)
         multiply(4)
         transposes(1, 0, 2)

@@ -30,6 +30,7 @@ OPENS = [sum(len(q) for q in PARTS[:i]) for i in range(len(PARTS))]
 CLOSES = [sum(len(q) for q in PARTS[: i + 1]) - 1 for i in range(len(PARTS))]
 STORES = [CLOSES[1], CLOSES[2]]
 PER_TICK = PASSES * N_TILES
+WARM_UPS = 8
 BEFORE = 10
 
 FLOPS = 2 * B * D * F * H
@@ -67,7 +68,12 @@ def tile_conditionembedder_w_e_kernel(
         nc.sync.dma_start(
             out=label_words[:], in_=labels.bitcast(I32).rearrange("(p t) w -> p (t w)", t=B_TILES)
         )
+        zeros = keep.tile([P, N_TILE], BF16)
+        nc.gpsimd.memset(zeros[:], 0.0)
         make_identity(nc, identity[:])
+        unread = acc_pool.tile([P, N_TILE], F32, name="acc0")
+        for k in range(WARM_UPS):
+            nc.tensor.matmul(out=unread[:], lhsT=zeros[:, 0:P], rhs=zeros[:], start=True, stop=True)
         nc.vector.memset(w_planes[:, 0, :].bitcast(I32), 0)
         nc.vector.memset(rows[:].bitcast(I32), 0)
         nc.scalar.dma_start(out=rows[0:D, :], in_=w1)
@@ -104,6 +110,19 @@ def tile_conditionembedder_w_e_kernel(
             op=ALU.add,
         )
 
+        magnitude = keep.tile([P, B_TILES * D], I32)
+        magnitude_pairs = magnitude[:].rearrange("p (w i) -> p w i", i=2)
+        nc.vector.tensor_scalar(
+            out=magnitude_pairs[:, :, 0],
+            in0=label_words[:],
+            scalar1=16,
+            scalar2=0x7FFFFFFF,
+            op0=ALU.logical_shift_left,
+            op1=ALU.bitwise_and,
+        )
+        nc.vector.tensor_single_scalar(
+            out=magnitude_pairs[:, :, 1], in_=label_words[:], scalar=0x7FFF0000, op=ALU.bitwise_and
+        )
         label_bits = keep.tile([P, B_TILES * D], I32)
         bit_pairs = label_bits[:].rearrange("p (w i) -> p w i", i=2)
         nc.vector.tensor_single_scalar(
@@ -111,10 +130,6 @@ def tile_conditionembedder_w_e_kernel(
         )
         nc.vector.tensor_single_scalar(
             out=bit_pairs[:, :, 1], in_=label_words[:], scalar=-65536, op=ALU.bitwise_and
-        )
-        magnitude = keep.tile([P, B_TILES * D], I32)
-        nc.vector.tensor_single_scalar(
-            out=magnitude[:], in_=label_bits[:], scalar=0x7FFFFFFF, op=ALU.bitwise_and
         )
         all_ones = keep.tile([P, B_TILES * D], I32)
         nc.vector.tensor_scalar(
@@ -125,18 +140,17 @@ def tile_conditionembedder_w_e_kernel(
             op0=ALU.is_le,
             op1=ALU.mult,
         )
-        safe_bits = keep.tile([P, B_TILES * D], I32)
-        nc.vector.tensor_tensor(
-            out=safe_bits[:], in0=label_bits[:], in1=all_ones[:], op=ALU.bitwise_and
+        present = keep.tile([P, B_TILES * D], F32)
+        nc.vector.tensor_single_scalar(
+            out=present[:], in_=magnitude[:], scalar=float(INFINITY_BITS), op=ALU.is_le
         )
 
         def by_tile(ap):
             return ap.rearrange("p (t d) -> p t d", t=B_TILES)
 
-        nc.vector.tensor_copy(out=columns[:, :, 0:D], in_=by_tile(safe_bits[:].bitcast(F32)))
-        present = keep.tile([P, B_TILES * D], F32)
-        nc.vector.tensor_single_scalar(
-            out=present[:], in_=magnitude[:], scalar=float(INFINITY_BITS), op=ALU.is_le
+        safe_bits = keep.tile([P, B_TILES * D], I32)
+        nc.vector.tensor_tensor(
+            out=safe_bits[:], in0=label_bits[:], in1=all_ones[:], op=ALU.bitwise_and
         )
         nc.vector.tensor_scalar(
             out=columns[:, :, ROW_EMB : ROW_EMB + D],
@@ -146,6 +160,7 @@ def tile_conditionembedder_w_e_kernel(
             op0=ALU.mult,
             op1=ALU.add,
         )
+        nc.vector.tensor_copy(out=columns[:, :, 0:D], in_=by_tile(safe_bits[:].bitcast(F32)))
         columns_t = tr_pool.tile([P, B_TILES, P], BF16, tag="tr")
         for t in range(B_TILES):
             nc.tensor.transpose(columns_t[:, t, :], columns[:, t, :], identity_bf[:])
@@ -311,8 +326,9 @@ def tile_conditionembedder_w_e_kernel(
         pending = []
         for u in range(len(UNITS)):
             if u == 0:
-                pending.extend((u, c, n) for c in range(PASSES) for n in (0, 1))
-                pending.extend((u, c, n) for c in range(PASSES) for n in (2, 3))
+                pending.extend((u, c, n) for c in (0, 1) for n in (0, 1))
+                pending.extend((u, c, n) for c in (0, 1) for n in (2, 3))
+                pending.extend((u, c, n) for c in (2, 3) for n in range(N_TILES))
             elif u in CLOSES:
                 pending.extend((u, c, n) for c in range(2) for n in range(N_TILES))
                 pending.extend((u, c, n) for n in range(N_TILES) for c in range(2, PASSES))
@@ -347,6 +363,10 @@ def tile_conditionembedder_w_e_kernel(
             cols = slice(n * N_TILE, (n + 1) * N_TILE)
             nc.scalar.copy(out=result[:, t, cols], in_=missing_banks[(t, n)][:])
 
+        def missing_copy_on_vector(t, n):
+            cols = slice(n * N_TILE, (n + 1) * N_TILE)
+            nc.vector.tensor_copy(out=result[:, t, cols], in_=missing_banks[(t, n)][:])
+
         stationary(D)
         for v in range(1, D):
             stationary_on_scalar(v)
@@ -363,19 +383,20 @@ def tile_conditionembedder_w_e_kernel(
         missing_product(0, 2)
         missing_copy(0, 2)
         missing_product(0, 3)
-        missing_copy(0, 3)
         evacuate(0, 2)
         evacuate(0, 3)
         row_maximum(0)
         exponentials(0)
+        missing_copy(0, 3)
         for c in range(PASSES):
             logits(1, c)
             evacuate(1, c)
+            if c < PASSES - 1:
+                missing_product(1, c)
         row_maximum(1)
         logits(2, 0)
         logits(2, 1)
-        for n in range(N_TILES):
-            missing_product(1, n)
+        missing_product(1, N_TILES - 1)
         missing_copy(1, 0)
         missing_copy(1, 1)
         normalise(0, 0, 1)
@@ -392,12 +413,13 @@ def tile_conditionembedder_w_e_kernel(
         quantise(0, 0, 1)
         quantise(0, 1, 2)
         multiply(4)
+        missing_copy_on_vector(1, 2)
+        missing_copy_on_vector(1, 3)
+        multiply(4)
         evacuate(2, 0)
         evacuate(2, 1)
         copies(0, 2, 3)
         copies(0, 3, 4)
-        missing_copy(1, 2)
-        missing_copy(1, 3)
         logits(2, 2)
         logits(2, 3)
         make_factor(1)
@@ -410,7 +432,7 @@ def tile_conditionembedder_w_e_kernel(
         transposes(1, 2, 4)
         copies(1, 0, 2)
         copies(1, 2, 4)
-        multiply(8)
+        multiply(4)
         evacuate(2, 2)
         evacuate(2, 3)
         row_maximum(2)

@@ -74,13 +74,13 @@ def tile_conditionembedder_w_e_kernel(
         unread = acc_pool.tile([P, N_TILE], F32, name="acc0")
         for k in range(WARM_UPS):
             nc.tensor.matmul(out=unread[:], lhsT=zeros[:, 0:P], rhs=zeros[:], start=True, stop=True)
-        nc.vector.memset(w_planes[:, 0, :].bitcast(I32), 0)
         nc.vector.memset(rows[:].bitcast(I32), 0)
-        nc.scalar.dma_start(out=rows[0:D, :], in_=w1)
-        nc.scalar.dma_start(out=rows[ROW_B1 : ROW_B1 + D, :], in_=b1)
-        nc.scalar.dma_start(out=rows[ROW_EMB : ROW_EMB + D, :], in_=emb_w)
+        nc.sync.dma_start(out=rows[0:D, :], in_=w1)
+        nc.sync.dma_start(out=rows[ROW_B1 : ROW_B1 + D, :], in_=b1)
+        nc.sync.dma_start(out=rows[ROW_EMB : ROW_EMB + D, :], in_=emb_w)
         nc.vector.memset(warm[:], 0.0)
         nc.scalar.activation(out=warm[:], in_=warm[:], func=ACT.Exp)
+        nc.vector.memset(w_planes[:, 0, :].bitcast(I32), 0)
 
         nc.vector.memset(w_planes[:, 1:D, :].rearrange("p d n -> p (d n)").bitcast(I32), 0)
         for d in range(D):

@@ -317,11 +317,18 @@ def tile_conditionembedder_w_e_kernel(
                 stop=last,
             )
             if last:
-                nc.vector.tensor_tensor(
-                    out=result[:, t, cols], in0=acc[n][:], in1=result[:, t, cols], op=ALU.add
-                )
-                if u in STORES:
-                    nc.sync.dma_start(out=out_rows[:, t, cols], in_=result[:, t, cols])
+                pieces = 2 if (u == len(UNITS) - 1 and n == N_TILES - 1) else 1
+                width = N_TILE // pieces
+                for piece in range(pieces):
+                    part = slice(n * N_TILE + piece * width, n * N_TILE + (piece + 1) * width)
+                    nc.vector.tensor_tensor(
+                        out=result[:, t, part],
+                        in0=acc[n][:, piece * width : (piece + 1) * width],
+                        in1=result[:, t, part],
+                        op=ALU.add,
+                    )
+                    if u in STORES:
+                        nc.sync.dma_start(out=out_rows[:, t, part], in_=result[:, t, part])
 
         pending = []
         for u in range(len(UNITS)):
@@ -437,7 +444,8 @@ def tile_conditionembedder_w_e_kernel(
         evacuate(2, 3)
         row_maximum(2)
         exponentials(2)
-        quantise(1, 0, PASSES)
+        quantise(1, 0, 2)
+        quantise(1, 2, PASSES)
         logits(3, 0)
         logits(3, 1)
 

from contextlib import ExitStack

import concourse.mybir as mybir
from concourse.masks import make_identity

F32 = mybir.dt.float32
BF16 = mybir.dt.bfloat16
I32 = mybir.dt.int32
U32 = mybir.dt.uint32
U8 = mybir.dt.uint8
FP8X4 = mybir.dt.float8_e4m3fn_x4
ALU = mybir.AluOpType
ACT = mybir.ActivationFunctionType

P = 128
B, D, F, H = 256, 4, 2048, 2048
B_TILES = B // P
K_PASS = 4 * P
PASSES = F // K_PASS
N_TILE = 512
N_TILES = H // N_TILE
INFINITY_BITS = 0x7F800000

ROW_B1 = D
ROW_EMB = 2 * D

PARTS = (((0, 0), (1, 0)), ((0, 1), (1, 1), (2, 1), (3, 1)), ((2, 0), (3, 0)))
UNITS = [unit for part in PARTS for unit in part]
OPENS = [sum(len(q) for q in PARTS[:i]) for i in range(len(PARTS))]
CLOSES = [sum(len(q) for q in PARTS[: i + 1]) - 1 for i in range(len(PARTS))]
STORES = [CLOSES[1], CLOSES[2]]
PER_TICK = PASSES * N_TILES
WARM_UPS = 8
BEFORE = 10

FLOPS = 2 * B * D * F * H


def tile_conditionembedder_w_e_kernel(
    tc, labels, emb_w, w1, b1, w2_words, w2_scales, train, unconditioned, out
):
    nc = tc.nc
    assert not train and not unconditioned

    with ExitStack() as ctx:
        keep = ctx.enter_context(tc.tile_pool(name="keep", bufs=1))
        work = ctx.enter_context(tc.tile_pool(name="work", bufs=2))
        small = ctx.enter_context(tc.tile_pool(name="small", bufs=4))
        acc_pool = ctx.enter_context(tc.psum_pool(name="acc", bufs=1))
        h1_pool = ctx.enter_context(tc.psum_pool(name="h1", bufs=2))
        tr_pool = ctx.enter_context(tc.psum_pool(name="tr", bufs=2))
        ctx.enter_context(tc.manual_schedule())

        rows = keep.tile([P, F], BF16)
        w_words = keep.tile([P, D * PASSES, H], U32, align_bytes=64)
        w_planes = keep.tile([P, D, H], U8, align_bytes=64)
        s_words = keep.tile([P, B_TILES, D * PASSES, P], U32, align_bytes=64)
        s_planes = keep.tile([P, B_TILES, D * PASSES, P], U8, align_bytes=64)
        result = keep.tile([P, B_TILES, H], F32)
        identity = keep.tile([P, P], F32)
        identity_bf = keep.tile([P, P], BF16)
        warm = keep.tile([P, 1], F32)
        label_words = keep.tile([P, B_TILES * D // 2], I32)
        columns = keep.tile([P, B_TILES, P], BF16)
        selectors = keep.tile([P, D + 1], F32)
        sample_rows = keep.tile([P, D + 1, B_TILES, P], BF16)

        nc.sync.dma_start(
            out=label_words[:], in_=labels.bitcast(I32).rearrange("(p t) w -> p (t w)", t=B_TILES)
        )
        zeros = keep.tile([P, N_TILE], BF16)
        nc.gpsimd.memset(zeros[:], 0.0)
        make_identity(nc, identity[:])
        unread = acc_pool.tile([P, N_TILE], F32, name="acc0")
        for k in range(WARM_UPS):
            nc.tensor.matmul(out=unread[:], lhsT=zeros[:, 0:P], rhs=zeros[:], start=True, stop=True)
        nc.vector.memset(rows[:].bitcast(I32), 0)
        nc.sync.dma_start(out=rows[0:D, :], in_=w1)
        nc.sync.dma_start(out=rows[ROW_B1 : ROW_B1 + D, :], in_=b1)
        nc.sync.dma_start(out=rows[ROW_EMB : ROW_EMB + D, :], in_=emb_w)
        nc.vector.memset(warm[:], 0.0)
        nc.scalar.activation(out=warm[:], in_=warm[:], func=ACT.Exp)
        nc.vector.memset(w_planes[:, 0, :].bitcast(I32), 0)

        nc.vector.memset(w_planes[:, 1:D, :].rearrange("p d n -> p (d n)").bitcast(I32), 0)
        for d in range(D):
            for quadrant in range(4):
                nc.sync.dma_start(
                    out=w_planes[32 * quadrant : 32 * quadrant + 16, d, :].bitcast(I32),
                    in_=w2_scales[
                        PASSES * d : PASSES * (d + 1), 4 * quadrant : 4 * quadrant + 4, :
                    ].bitcast(I32),
                )
            for g in range(PASSES * d, PASSES * (d + 1)):
                nc.sync.dma_start(
                    out=w_words[:, g, :].bitcast(I32),
                    in_=w2_words[g].rearrange("p n t -> p (n t)").bitcast(I32),
                )

        nc.vector.memset(columns[:].rearrange("p t k -> p (t k)").bitcast(I32), 0)
        nc.vector.memset(columns[:, :, ROW_B1 : ROW_B1 + D], 1.0)
        nc.vector.tensor_copy(out=identity_bf[:], in_=identity[:])
        nc.vector.tensor_tensor(
            out=selectors[:, 0:D], in0=identity[:, 0:D], in1=identity[:, ROW_B1 : ROW_B1 + D], op=ALU.add
        )
        nc.vector.tensor_reduce(
            out=selectors[:, D : D + 1],
            in_=identity[:, ROW_EMB : ROW_EMB + D],
            axis=mybir.AxisListType.X,
            op=ALU.add,
        )

        magnitude = keep.tile([P, B_TILES * D], I32)
        magnitude_pairs = magnitude[:].rearrange("p (w i) -> p w i", i=2)
        nc.vector.tensor_scalar(
            out=magnitude_pairs[:, :, 0],
            in0=label_words[:],
            scalar1=16,
            scalar2=0x7FFFFFFF,
            op0=ALU.logical_shift_left,
            op1=ALU.bitwise_and,
        )
        nc.vector.tensor_single_scalar(
            out=magnitude_pairs[:, :, 1], in_=label_words[:], scalar=0x7FFF0000, op=ALU.bitwise_and
        )
        label_bits = keep.tile([P, B_TILES * D], I32)
        bit_pairs = label_bits[:].rearrange("p (w i) -> p w i", i=2)
        nc.vector.tensor_single_scalar(
            out=bit_pairs[:, :, 0], in_=label_words[:], scalar=16, op=ALU.logical_shift_left
        )
        nc.vector.tensor_single_scalar(
            out=bit_pairs[:, :, 1], in_=label_words[:], scalar=-65536, op=ALU.bitwise_and
        )
        all_ones = keep.tile([P, B_TILES * D], I32)
        nc.vector.tensor_scalar(
            out=all_ones[:],
            in0=magnitude[:],
            scalar1=float(INFINITY_BITS),
            scalar2=-1.0,
            op0=ALU.is_le,
            op1=ALU.mult,
        )
        present = keep.tile([P, B_TILES * D], F32)
        nc.vector.tensor_single_scalar(
            out=present[:], in_=magnitude[:], scalar=float(INFINITY_BITS), op=ALU.is_le
        )

        def by_tile(ap):
            return ap.rearrange("p (t d) -> p t d", t=B_TILES)

        safe_bits = keep.tile([P, B_TILES * D], I32)
        nc.vector.tensor_tensor(
            out=safe_bits[:], in0=label_bits[:], in1=all_ones[:], op=ALU.bitwise_and
        )
        nc.vector.tensor_scalar(
            out=columns[:, :, ROW_EMB : ROW_EMB + D],
            in0=by_tile(present[:]),
            scalar1=-1.0,
            scalar2=1.0,
            op0=ALU.mult,
            op1=ALU.add,
        )
        nc.vector.tensor_copy(out=columns[:, :, 0:D], in_=by_tile(safe_bits[:].bitcast(F32)))
        columns_t = tr_pool.tile([P, B_TILES, P], BF16, tag="tr")
        for t in range(B_TILES):
            nc.tensor.transpose(columns_t[:, t, :], columns[:, t, :], identity_bf[:])

        def stationary(v):
            nc.vector.tensor_scalar_mul(
                out=sample_rows[:, v, :, :].rearrange("k t b -> k (t b)"),
                in0=columns_t[:].rearrange("k t b -> k (t b)"),
                scalar1=selectors[:, v : v + 1],
            )

        def stationary_on_scalar(v):
            nc.scalar.activation(
                out=sample_rows[:, v, :, :].rearrange("k t b -> k (t b)"),
                in_=columns_t[:].rearrange("k t b -> k (t b)"),
                func=ACT.Copy,
                scale=selectors[:, v : v + 1],
            )

        stationary(0)

        e_tiles, max_tiles, sum_tiles, s_tiles, factors, grouped_tiles, banks, h1_tiles = {}, {}, {}, {}, {}, {}, {}, {}

        def logits(u, c):
            d, t = UNITS[u]
            run = slice(c * K_PASS, (c + 1) * K_PASS)
            h1_tiles[(u, c)] = h1_pool.tile([P, K_PASS], F32, name="h1")
            nc.tensor.matmul(
                out=h1_tiles[(u, c)][:], lhsT=sample_rows[:, d, t, :], rhs=rows[:, run], start=True, stop=True
            )

        def evacuate(u, c):
            if c == 0:
                e_tiles[u] = work.tile([P, F], F32, name="e")
                max_tiles[u] = small.tile([P, PASSES], F32, name="run_max")
            run = slice(c * K_PASS, (c + 1) * K_PASS)
            h1 = h1_tiles[(u, c)]
            nc.vector.tensor_scalar(
                out=e_tiles[u][:, run].rearrange("b (u p i) -> b u p i", u=2, i=2),
                in0=h1[:].rearrange("b (p u i) -> b u p i", u=2, i=2),
                scalar1=1.0,
                scalar2=None,
                op0=ALU.mult,
                op1=ALU.max,
                accum_out=max_tiles[u][:, c : c + 1],
            )

        def row_maximum(u):
            minus_max = small.tile([P, 1], F32)
            nc.vector.tensor_reduce(
                out=minus_max[:],
                in_=max_tiles[u][:],
                axis=mybir.AxisListType.X,
                op=ALU.max,
                negate=True,
            )
            max_tiles[u] = minus_max

        def exponentials(u):
            sum_tiles[u] = small.tile([P, 1], F32, name="total")
            nc.scalar.activation(
                out=e_tiles[u][:],
                in_=e_tiles[u][:],
                func=ACT.Exp,
                bias=max_tiles[u][:],
                scale=1.0,
                accum_out=sum_tiles[u][:],
            )

        def make_factor(u):
            d, t = UNITS[u]
            factor = small.tile([P, 1], F32)
            nc.vector.reciprocal(out=factor[:], in_=sum_tiles[u][:])
            column = t * D + d
            nc.vector.tensor_mul(out=factor[:], in0=factor[:], in1=present[:, column : column + 1])
            factors[u] = factor

        def normalise(u, first, last):
            if first == 0:
                if u not in factors:
                    make_factor(u)
                s_tiles[u] = work.tile([P, F], BF16, name="s")
            cols = slice(first * K_PASS, last * K_PASS)
            nc.vector.tensor_scalar_mul(
                out=s_tiles[u][:, cols], in0=e_tiles[u][:, cols], scalar1=factors[u][:]
            )

        def normalise_on_scalar(u, first, last):
            cols = slice(first * K_PASS, last * K_PASS)
            nc.scalar.activation(
                out=s_tiles[u][:, cols], in_=e_tiles[u][:, cols], func=ACT.Copy, scale=factors[u][:]
            )

        def transposes(u, first, last):
            s_pairs = s_tiles[u][:].bitcast(F32)
            for c in range(first, last):
                if (c - first) % 2 == 0:
                    banks[(u, c)] = tr_pool.tile([P, 2, 2, P], F32, name="tr")
                else:
                    banks[(u, c)] = banks[(u, c - 1)]
                for pair in range(2):
                    begin = (c * 2 + pair) * P
                    nc.tensor.transpose(
                        banks[(u, c)][:, (c - first) % 2, pair, :], s_pairs[:, begin : begin + P], identity[:]
                    )

        def copies(u, first, last):
            if first == 0:
                grouped_tiles[u] = work.tile([P, PASSES, P, 4], BF16, name="grouped", align_bytes=64)
            grouped_pairs = (
                grouped_tiles[u][:]
                .rearrange("p c b j -> p (c b j)")
                .bitcast(F32)
                .rearrange("p (c b u) -> p c b u", c=PASSES, u=2)
            )
            for c in range(first, last, 2):
                count = min(2, last - c)
                nc.scalar.copy(
                    out=grouped_pairs[:, c : c + count],
                    in_=banks[(u, c)][:, 0:count].rearrange("p c u b -> p c b u"),
                )

        quantised = set()

        def quantise(u, first, last):
            d, t = UNITS[u]
            passes = slice(PASSES * d + first, PASSES * d + last)
            nc.vector.quantize_mx(
                out=s_words[:, t, passes, :].rearrange("p g b -> p (g b)").bitcast(FP8X4),
                scales=s_planes[:, t, passes, :].rearrange("p g b -> p (g b)"),
                in_=grouped_tiles[u][:, first:last].rearrange("p c b j -> p (c b j)"),
            )
            for c in range(first, last):
                quantised.add((u, c))

        acc = {}
        out_rows = out.rearrange("(p t) n -> p t n", t=B_TILES)

        def one_pass(u, c, n):
            d, t = UNITS[u]
            g = PASSES * d + c
            cols = slice(n * N_TILE, (n + 1) * N_TILE)
            first = u in OPENS and c == 0
            last = u in CLOSES and c == PASSES - 1
            if first:
                acc[n] = acc_pool.tile([P, N_TILE], F32, name="acc%d" % n)
            nc.tensor.matmul_mx(
                out=acc[n][:],
                lhsT=s_words[:, t, g, :].bitcast(FP8X4),
                lhsT_scale=s_planes[:, t, g, :],
                rhs=w_words[:, g, cols].bitcast(FP8X4),
                rhs_scale=w_planes[4 * c : P, d, cols],
                start=first,
                stop=last,
            )
            if last:
                pieces = 2 if (u == len(UNITS) - 1 and n == N_TILES - 1) else 1
                width = N_TILE // pieces
                for piece in range(pieces):
                    part = slice(n * N_TILE + piece * width, n * N_TILE + (piece + 1) * width)
                    nc.vector.tensor_tensor(
                        out=result[:, t, part],
                        in0=acc[n][:, piece * width : (piece + 1) * width],
                        in1=result[:, t, part],
                        op=ALU.add,
                    )
                    if u in STORES:
                        nc.sync.dma_start(out=out_rows[:, t, part], in_=result[:, t, part])

        pending = []
        for u in range(len(UNITS)):
            if u == 0:
                pending.extend((u, c, n) for c in (0, 1) for n in (0, 1))
                pending.extend((u, c, n) for c in (0, 1) for n in (2, 3))
                pending.extend((u, c, n) for c in (2, 3) for n in range(N_TILES))
            elif u in CLOSES:
                pending.extend((u, c, n) for c in range(2) for n in range(N_TILES))
                pending.extend((u, c, n) for n in range(N_TILES) for c in range(2, PASSES))
            else:
                pending.extend((u, c, n) for c in range(PASSES) for n in range(N_TILES))
        done = []

        def multiply(count):
            for k in range(count):
                if len(done) == len(pending) or pending[len(done)][0:2] not in quantised:
                    return
                one_pass(*pending[len(done)])
                done.append(1)

        def missing_term(t, n, pool_tile):
            cols = slice(n * N_TILE, (n + 1) * N_TILE)
            nc.tensor.matmul(
                out=pool_tile[:], lhsT=sample_rows[:, D, t, :], rhs=rows[:, cols], start=True, stop=True
            )
            return cols

        def valid(u):
            return 0 <= u < len(UNITS)

        missing_banks = {}

        def missing_product(t, n):
            missing_banks[(t, n)] = acc_pool.tile([P, N_TILE], F32, name="acc%d" % n)
            missing_term(t, n, missing_banks[(t, n)])

        def missing_copy(t, n):
            cols = slice(n * N_TILE, (n + 1) * N_TILE)
            nc.scalar.copy(out=result[:, t, cols], in_=missing_banks[(t, n)][:])

        def missing_copy_on_vector(t, n):
            cols = slice(n * N_TILE, (n + 1) * N_TILE)
            nc.vector.tensor_copy(out=result[:, t, cols], in_=missing_banks[(t, n)][:])

        stationary(D)
        for v in range(1, D):
            stationary_on_scalar(v)
        logits(0, 0)
        logits(0, 1)
        evacuate(0, 0)
        evacuate(0, 1)
        missing_product(0, 0)
        missing_copy(0, 0)
        logits(0, 2)
        missing_product(0, 1)
        missing_copy(0, 1)
        logits(0, 3)
        missing_product(0, 2)
        missing_copy(0, 2)
        missing_product(0, 3)
        evacuate(0, 2)
        evacuate(0, 3)
        row_maximum(0)
        exponentials(0)
        missing_copy(0, 3)
        for c in range(PASSES):
            logits(1, c)
            evacuate(1, c)
            if c < PASSES - 1:
                missing_product(1, c)
        row_maximum(1)
        logits(2, 0)
        logits(2, 1)
        missing_product(1, N_TILES - 1)
        missing_copy(1, 0)
        missing_copy(1, 1)
        normalise(0, 0, 1)
        transposes(0, 0, 1)
        copies(0, 0, 1)
        normalise(0, 1, 2)
        transposes(0, 1, 2)
        copies(0, 1, 2)
        exponentials(1)
        normalise(0, 2, 3)
        transposes(0, 2, 3)
        normalise(0, 3, 4)
        transposes(0, 3, 4)
        quantise(0, 0, 1)
        quantise(0, 1, 2)
        multiply(4)
        missing_copy_on_vector(1, 2)
        missing_copy_on_vector(1, 3)
        multiply(4)
        evacuate(2, 0)
        evacuate(2, 1)
        copies(0, 2, 3)
        copies(0, 3, 4)
        logits(2, 2)
        logits(2, 3)
        make_factor(1)
        quantise(0, 2, 3)
        quantise(0, 3, 4)
        normalise(1, 0, 2)
        normalise(1, 2, 4)
        multiply(4)
        transposes(1, 0, 2)
        transposes(1, 2, 4)
        copies(1, 0, 2)
        copies(1, 2, 4)
        multiply(4)
        evacuate(2, 2)
        evacuate(2, 3)
        row_maximum(2)
        exponentials(2)
        quantise(1, 0, 2)
        quantise(1, 2, PASSES)
        logits(3, 0)
        logits(3, 1)

        for a in range(3, len(UNITS) + 1):
            if valid(a):
                evacuate(a, 0)
                evacuate(a, 1)
            normalise(a - 1, 0, 2)
            normalise_on_scalar(a - 1, 2, PASSES)
            multiply(BEFORE)
            if valid(a):
                logits(a, 2)
                logits(a, 3)
            transposes(a - 1, 0, PASSES)
            copies(a - 1, 0, PASSES)
            if valid(a):
                evacuate(a, 2)
                evacuate(a, 3)
                row_maximum(a)
                exponentials(a)
            quantise(a - 1, 0, PASSES)
            multiply(PER_TICK - BEFORE)
            if valid(a + 1):
                logits(a + 1, 0)
                logits(a + 1, 1)
        multiply(len(pending))
